import numpy as np
import ml_dtypes


def mxq(x, axis, fmt="e4m3"):
    dtype, down = {"e4m3": (ml_dtypes.float8_e4m3fn, 7), "e5m2": (ml_dtypes.float8_e5m2, 14)}[fmt]
    v = np.moveaxis(np.asarray(x, np.float32).astype(ml_dtypes.bfloat16).astype(np.float64), axis, -1)
    blocks = v.reshape(v.shape[:-1] + (-1, 32))
    amax = np.abs(blocks).max(-1, keepdims=True)
    byte = np.maximum(np.where(amax > 0, np.frexp(amax)[1] - 1 + 127, 0) - down, 1)
    scale = np.exp2(byte - 127.0)
    codes = (blocks / scale).astype(np.float32).astype(dtype).astype(np.float64)
    return np.moveaxis((codes * scale).reshape(v.shape), -1, axis)


WIDE = False


def mx_kscale(k):
    if not WIDE:
        return np.ones(k)
    levels = np.array([10, -10, 5, -5, 0])
    a = np.random.permutation(np.resize(levels, k // 512 * 4)).reshape(k // 512, 4)
    idx = np.arange(k)
    return np.exp2(a[idx // 512, idx % 128 // 32])


BF16 = ml_dtypes.bfloat16


def bf(x):
    return np.asarray(x, np.float32).astype(BF16)


def f64(x):
    return np.asarray(x).astype(np.float64)


B, N, D, E, M, R = 16, 1024, 512, 128, 4096, 4
EPS = 1e-6


def layer_norm(v, g, b):
    mu = v.mean(-1, keepdims=True)
    var = ((v - mu) ** 2).mean(-1, keepdims=True)
    return (v - mu) / np.sqrt(var + EPS) * g + b


def merge(t):
    return t.reshape(B, N // R, R, E).mean(axis=2)


def setup_inputs():
    s = mx_kscale(D)

    def w():
        return bf(np.random.standard_normal((E, D)) * 2.0 / np.sqrt(D) / s)

    def c():
        return bf(np.random.standard_normal(E) * 0.3)

    x = np.random.standard_normal((B, N, D)) * (0.5 + 1.5 * np.random.random((B, N, 1))) + np.random.standard_normal((B, N, 1))
    return {"x": bf(x),
            "ln1_g": bf((1.0 + 0.1 * np.random.standard_normal(D)) * s),
            "ln1_b": bf(0.1 * np.random.standard_normal(D) * s),
            "Wq": w(), "bq": c(), "Wk": w(), "bk": c(), "Wv": w(), "bv": c()}


def reference(x, ln1_g, ln1_b, Wq, bq, Wk, bk, Wv, bv):
    h = layer_norm(f64(x), f64(ln1_g), f64(ln1_b))
    hq = mxq(h, 2, "e4m3")
    Q = (hq @ mxq(f64(Wq), 1, "e4m3").T) + f64(bq)
    K = (hq @ mxq(f64(Wk), 1, "e4m3").T) + f64(bk)
    V = (hq @ mxq(f64(Wv), 1, "e4m3").T) + f64(bv)
    return Q, merge(K), merge(V)

@@ -1,0 +1,228 @@
+from contextlib import ExitStack
+
+import concourse.mybir as mybir
+from concourse.masks import make_identity
+
+F32 = mybir.dt.float32
+BF16 = mybir.dt.bfloat16
+U32 = mybir.dt.uint32
+U8 = mybir.dt.uint8
+FP8X4 = mybir.dt.float8_e4m3fn_x4
+ACT = mybir.ActivationFunctionType
+ALU = mybir.AluOpType
+
+P = 128
+PACK = 4
+TOKENS = 16 * 1024
+D = P * PACK
+E = 128
+MERGE = 4
+EPS = 1e-6
+GROUP = P * MERGE
+GROUPS = TOKENS // GROUP
+RUN = 4
+AHEAD = 3
+
+FLOPS = 2 * TOKENS * D * 3 * E
+
+
+def tile_siglipencoderlayer_pa_t_kernel(
+    tc, x, ln1_g, ln1_b, Wq, bq, Wk, bk, Wv, bv, out_0, out_1, out_2
+):
+    nc = tc.nc
+    with ExitStack() as ctx:
+        keep = ctx.enter_context(tc.tile_pool(name="keep", bufs=1))
+
+        ident_f32 = keep.tile([P, P], F32)
+        make_identity(nc, ident_f32[:])
+        ident_bf16 = keep.tile([P, P], BF16)
+        make_identity(nc, ident_bf16[:])
+        eps_col = keep.tile([P, 1], F32)
+        nc.vector.memset(eps_col[:], EPS)
+
+        w_rows = keep.tile([P, 3, D], BF16)
+        for w, weight in enumerate((Wq, Wk, Wv)):
+            nc.scalar.dma_start(out=w_rows[:, w, :], in_=weight)
+        gb_rows = keep.tile([P, P], BF16)
+        nc.vector.memset(gb_rows[:], 0.0)
+        nc.scalar.dma_start(out=gb_rows[0:PACK, :], in_=ln1_g.rearrange("(c p) -> c p", p=P))
+        nc.scalar.dma_start(out=gb_rows[PACK : 2 * PACK, :], in_=ln1_b.rearrange("(c p) -> c p", p=P))
+        bias_bf16 = keep.tile([P, 3, E], BF16)
+        for w, bias in enumerate((bq, bk, bv)):
+            nc.scalar.dma_start(out=bias_bf16[:, w, :], in_=bias.partition_broadcast(P))
+        bias_f32 = keep.tile([P, 3, E], F32)
+        nc.vector.tensor_copy(out=bias_f32[:], in_=bias_bf16[:])
+
+        w_grouped = keep.tile([P, 3, E, PACK], BF16, align_bytes=64)
+        w_codes = keep.tile([P, 3 * E], U32, align_bytes=64)
+        w_scales = keep.tile([P, 3 * E], U8, align_bytes=64)
+        gb_cols = keep.tile([P, 2 * PACK], F32)
+        with tc.psum_pool(name="setup_psum", bufs=1) as setup_psum:
+            gb_t = setup_psum.tile([P, P], BF16)
+            nc.tensor.transpose(gb_t[:], gb_rows[:], ident_bf16[:])
+            nc.vector.tensor_copy(out=gb_cols[:], in_=gb_t[:, 0 : 2 * PACK])
+            for w in range(3):
+                w_t = setup_psum.tile([P, PACK, E], BF16, tag="w_t", bufs=2)
+                for c in range(PACK):
+                    nc.tensor.transpose(w_t[:, c, :], w_rows[:, w, c * P : (c + 1) * P], ident_bf16[:])
+                nc.vector.tensor_copy(out=w_grouped[:, w], in_=w_t[:].rearrange("p c e -> p e c"))
+        nc.vector.quantize_mx(
+            out=w_codes[:, 0:E].bitcast(FP8X4),
+            scales=w_scales[:, 0:E],
+            in_=w_grouped[:, 0].rearrange("p e c -> p (e c)"),
+        )
+        nc.vector.quantize_mx(
+            out=w_codes[:, E : 3 * E].bitcast(FP8X4),
+            scales=w_scales[:, E : 3 * E],
+            in_=w_grouped[:, 1:3].rearrange("p w e c -> p (w e c)"),
+        )
+
+        x_view = x.flatten_outer_dims().rearrange("(g p r) d -> g p r d", p=P, r=MERGE)
+        q_view = out_0.flatten_outer_dims().rearrange("(g p r) e -> g p r e", p=P, r=MERGE)
+        k_view = out_1.flatten_outer_dims().rearrange("(g p) e -> g p e", p=P)
+        v_view = out_2.flatten_outer_dims().rearrange("(g p) e -> g p e", p=P)
+
+        x_pool = ctx.enter_context(tc.tile_pool(name="x_pool", bufs=AHEAD + 4))
+        stat_pool = ctx.enter_context(tc.tile_pool(name="stat_pool", bufs=4))
+        work = ctx.enter_context(tc.tile_pool(name="work", bufs=3))
+        t_psum = ctx.enter_context(tc.psum_pool(name="t_psum", bufs=1))
+        o_psum = ctx.enter_context(tc.psum_pool(name="o_psum", bufs=2))
+
+        x_of, stats_of, moments_of, std_of, rstd_of, neg_mean_of = {}, {}, {}, {}, {}, {}
+        y_of, y_t_of, planes_of, grouped_of, codes_of, scales_of, q_ps_of, kv_ps_of = {}, {}, {}, {}, {}, {}, {}, {}
+
+        def load(g):
+            x_sb = x_pool.tile([P, MERGE, D], BF16)
+            nc.sync.dma_start(out=x_sb[:], in_=x_view[g])
+            x_of[g] = x_sb
+
+        def statistics(g):
+            stats = stat_pool.tile([P, MERGE, 6], F32)
+            for r in range(MERGE):
+                nc.vector.bn_stats(out=stats[:, r, :], in_=x_of[g][:, r, :])
+            stats_of[g] = stats
+
+        def aggregate(g):
+            moments = stat_pool.tile([P, MERGE, 2], F32)
+            for r in range(MERGE):
+                nc.vector.bn_aggr(out=moments[:, r, :], in_=stats_of[g][:, r, :])
+            moments_of[g] = moments
+
+        def deviation(g):
+            std = stat_pool.tile([P, MERGE], F32)
+            nc.scalar.activation(out=std[:], in_=moments_of[g][:, :, 1], func=ACT.Sqrt, bias=eps_col[:], scale=1.0)
+            std_of[g] = std
+            neg_mean = stat_pool.tile([P, MERGE], F32)
+            nc.gpsimd.tensor_scalar(
+                out=neg_mean[:], in0=moments_of[g][:, :, 0], scalar1=-1.0, scalar2=0.0, op0=ALU.mult, op1=ALU.add
+            )
+            neg_mean_of[g] = neg_mean
+
+        def inverse(g):
+            rstd = stat_pool.tile([P, MERGE], F32)
+            nc.vector.reciprocal(out=rstd[:], in_=std_of[g][:])
+            rstd_of[g] = rstd
+
+        def normalise(g):
+            y = work.tile([P, MERGE, D], F32)
+            for r in range(MERGE):
+                nc.gpsimd.tensor_scalar(
+                    out=y[:, r, :], in0=x_of[g][:, r, :],
+                    scalar1=neg_mean_of[g][:, r : r + 1], scalar2=rstd_of[g][:, r : r + 1],
+                    op0=ALU.add, op1=ALU.mult,
+                )
+            y_of[g] = y
+
+        def transpose(g):
+            y_t = [t_psum.tile([P, MERGE, P], F32, name="y_t%d" % c) for c in range(PACK)]
+            for c in range(PACK):
+                for r in range(MERGE):
+                    nc.tensor.transpose(y_t[c][:, r, :], y_of[g][:, r, c * P : (c + 1) * P], ident_f32[:])
+            y_t_of[g] = y_t
+
+        def scale_shift(g):
+            planes = work.tile([P, PACK, GROUP], BF16)
+            for c in range(PACK):
+                nc.scalar.activation(
+                    out=planes[:, c, :], in_=y_t_of[g][c][:].rearrange("p r t -> p (r t)"), func=ACT.Identity,
+                    scale=gb_cols[:, c : c + 1], bias=gb_cols[:, PACK + c : PACK + c + 1],
+                )
+            planes_of[g] = planes
+
+        def regroup(g):
+            planes = planes_of[g]
+            grouped = work.tile([P, GROUP, PACK], BF16, align_bytes=64)
+            nc.vector.tensor_copy(
+                out=grouped[:, 0:P, :].rearrange("p (a i) c -> p a c i", i=RUN),
+                in_=planes[:, :, 0:P].rearrange("p c (a i) -> p a c i", i=RUN),
+            )
+            nc.scalar.copy(
+                out=grouped[:, P:, :].rearrange("p (a i) c -> p a c i", i=RUN),
+                in_=planes[:, :, P:].rearrange("p c (a i) -> p a c i", i=RUN),
+            )
+            grouped_of[g] = grouped
+
+        def quantise(g):
+            h_codes = work.tile([P, GROUP], U32, align_bytes=64)
+            h_scales = work.tile([P, GROUP], U8, align_bytes=64)
+            nc.vector.quantize_mx(
+                out=h_codes[:].bitcast(FP8X4), scales=h_scales[:],
+                in_=grouped_of[g][:].rearrange("p t c -> p (t c)"),
+            )
+            codes_of[g] = h_codes
+            scales_of[g] = h_scales
+
+        def project(g):
+            q_ps = o_psum.tile([P, MERGE, E], F32)
+            kv_ps = o_psum.tile([P, 2, E], F32)
+            for r in range(MERGE):
+                cols = slice(r * P, (r + 1) * P)
+                nc.tensor.matmul_mx(
+                    out=q_ps[:, r, :],
+                    lhsT=codes_of[g][:, cols].bitcast(FP8X4), lhsT_scale=scales_of[g][:, cols],
+                    rhs=w_codes[:, 0:E].bitcast(FP8X4), rhs_scale=w_scales[:, 0:E],
+                    start=True, stop=True,
+                )
+                nc.tensor.matmul_mx(
+                    out=kv_ps[:].rearrange("p s e -> p (s e)"),
+                    lhsT=codes_of[g][:, cols].bitcast(FP8X4), lhsT_scale=scales_of[g][:, cols],
+                    rhs=w_codes[:, E : 3 * E].bitcast(FP8X4), rhs_scale=w_scales[:, E : 3 * E],
+                    start=(r == 0), stop=(r == MERGE - 1),
+                )
+            q_ps_of[g] = q_ps
+            kv_ps_of[g] = kv_ps
+
+        def finish(g):
+            q_sb = work.tile([P, MERGE, E], F32)
+            nc.vector.tensor_tensor(
+                out=q_sb[:], in0=q_ps_of[g][:], in1=bias_f32[:, 0:1, :].to_broadcast([P, MERGE, E]), op=ALU.add
+            )
+            kv_sb = work.tile([P, 2, E], F32)
+            nc.vector.scalar_tensor_tensor(
+                out=kv_sb[:], in0=kv_ps_of[g][:], scalar=1.0 / MERGE, in1=bias_f32[:, 1:3, :],
+                op0=ALU.mult, op1=ALU.add,
+            )
+            nc.sync.dma_start(out=q_view[g], in_=q_sb[:])
+            nc.sync.dma_start(out=k_view[g], in_=kv_sb[:, 0])
+            nc.sync.dma_start(out=v_view[g], in_=kv_sb[:, 1])
+
+        def run(stage, g):
+            if 0 <= g < GROUPS:
+                stage(g)
+
+        with tc.manual_schedule():
+            for g in range(AHEAD):
+                load(g)
+            for t in range(GROUPS + 7):
+                run(load, t + AHEAD)
+                run(finish, t - 6)
+                run(regroup, t - 4)
+                run(transpose, t - 3)
+                run(statistics, t)
+                run(deviation, t - 1)
+                run(inverse, t - 1)
+                run(aggregate, t)
+                run(normalise, t - 2)
+                run(scale_shift, t - 3)
+                run(quantise, t - 4)
+                run(project, t - 5)

@@ -11,6 +11,8 @@ FP8X4 = mybir.dt.float8_e4m3fn_x4
 ACT = mybir.ActivationFunctionType
 ALU = mybir.AluOpType
 
+I32 = mybir.dt.int32
+
 P = 128
 PACK = 4
 TOKENS = 16 * 1024
@@ -22,6 +24,11 @@ GROUP = P * MERGE
 GROUPS = TOKENS // GROUP
 RUN = 4
 AHEAD = 3
+VECTOR_SHARE = P
+SCALAR_SHARE = (GROUP - VECTOR_SHARE) // 2
+KV_FROM, KV_TO = 0, 4
+PREPARE_ROUND = 2
+LAST_LAG = 8
 
 FLOPS = 2 * TOKENS * D * 3 * E
 
@@ -32,6 +39,11 @@ def tile_siglipencoderlayer_pa_t_kernel(
     nc = tc.nc
     with ExitStack() as ctx:
         keep = ctx.enter_context(tc.tile_pool(name="keep", bufs=1))
+        x_pool = ctx.enter_context(tc.tile_pool(name="x_pool", bufs=AHEAD + 4))
+        stat_pool = ctx.enter_context(tc.tile_pool(name="stat_pool", bufs=4))
+        work = ctx.enter_context(tc.tile_pool(name="work", bufs=3))
+        t_psum = ctx.enter_context(tc.psum_pool(name="t_psum", bufs=1))
+        o_psum = ctx.enter_context(tc.psum_pool(name="o_psum", bufs=2))
 
         ident_f32 = keep.tile([P, P], F32)
         make_identity(nc, ident_f32[:])
@@ -41,52 +53,51 @@ def tile_siglipencoderlayer_pa_t_kernel(
         nc.vector.memset(eps_col[:], EPS)
 
         w_rows = keep.tile([P, 3, D], BF16)
-        for w, weight in enumerate((Wq, Wk, Wv)):
-            nc.scalar.dma_start(out=w_rows[:, w, :], in_=weight)
         gb_rows = keep.tile([P, P], BF16)
         nc.vector.memset(gb_rows[:], 0.0)
-        nc.scalar.dma_start(out=gb_rows[0:PACK, :], in_=ln1_g.rearrange("(c p) -> c p", p=P))
-        nc.scalar.dma_start(out=gb_rows[PACK : 2 * PACK, :], in_=ln1_b.rearrange("(c p) -> c p", p=P))
         bias_bf16 = keep.tile([P, 3, E], BF16)
-        for w, bias in enumerate((bq, bk, bv)):
-            nc.scalar.dma_start(out=bias_bf16[:, w, :], in_=bias.partition_broadcast(P))
         bias_f32 = keep.tile([P, 3, E], F32)
-        nc.vector.tensor_copy(out=bias_f32[:], in_=bias_bf16[:])
-
         w_grouped = keep.tile([P, 3, E, PACK], BF16, align_bytes=64)
-        w_codes = keep.tile([P, 3 * E], U32, align_bytes=64)
-        w_scales = keep.tile([P, 3 * E], U8, align_bytes=64)
+        w_codes = keep.tile([P, 4 * E], U32, align_bytes=64)
+        w_scales = keep.tile([P, 4 * E], U8, align_bytes=64)
+        nc.vector.memset(w_codes[:, 3 * E :].bitcast(I32), 0)
+        nc.vector.memset(w_scales[:, 3 * E :].bitcast(I32), 0)
         gb_cols = keep.tile([P, 2 * PACK], F32)
-        with tc.psum_pool(name="setup_psum", bufs=1) as setup_psum:
-            gb_t = setup_psum.tile([P, P], BF16)
+
+        def load_parameters():
+            nc.sync.dma_start(out=gb_rows[0:PACK, :], in_=ln1_g.rearrange("(c p) -> c p", p=P))
+            nc.sync.dma_start(out=gb_rows[PACK : 2 * PACK, :], in_=ln1_b.rearrange("(c p) -> c p", p=P))
+            for w, weight in enumerate((Wq, Wk, Wv)):
+                nc.sync.dma_start(out=w_rows[:, w, :], in_=weight)
+
+        def load_biases():
+            for w, bias in enumerate((bq, bk, bv)):
+                nc.sync.dma_start(out=bias_bf16[:, w, :], in_=bias.partition_broadcast(P))
+
+        def prepare_parameters():
+            gb_t = o_psum.tile([P, P], BF16, tag="q_ps")
             nc.tensor.transpose(gb_t[:], gb_rows[:], ident_bf16[:])
+            w_t = [o_psum.tile([P, PACK, E], BF16, name="w_t%d" % w, tag=("q_ps", "kv_ps", "kv_ps")[w]) for w in range(3)]
+            for w in range(3):
+                for c in range(PACK):
+                    nc.tensor.transpose(w_t[w][:, c, :], w_rows[:, w, c * P : (c + 1) * P], ident_bf16[:])
             nc.vector.tensor_copy(out=gb_cols[:], in_=gb_t[:, 0 : 2 * PACK])
             for w in range(3):
-                w_t = setup_psum.tile([P, PACK, E], BF16, tag="w_t", bufs=2)
-                for c in range(PACK):
-                    nc.tensor.transpose(w_t[:, c, :], w_rows[:, w, c * P : (c + 1) * P], ident_bf16[:])
-                nc.vector.tensor_copy(out=w_grouped[:, w], in_=w_t[:].rearrange("p c e -> p e c"))
-        nc.vector.quantize_mx(
-            out=w_codes[:, 0:E].bitcast(FP8X4),
-            scales=w_scales[:, 0:E],
-            in_=w_grouped[:, 0].rearrange("p e c -> p (e c)"),
-        )
-        nc.vector.quantize_mx(
-            out=w_codes[:, E : 3 * E].bitcast(FP8X4),
-            scales=w_scales[:, E : 3 * E],
-            in_=w_grouped[:, 1:3].rearrange("p w e c -> p (w e c)"),
-        )
+                nc.vector.tensor_copy(out=w_grouped[:, w], in_=w_t[w][:].rearrange("p c e -> p e c"))
+            nc.vector.tensor_copy(out=bias_f32[:], in_=bias_bf16[:])
+            nc.vector.quantize_mx(
+                out=w_codes[:, 0:E].bitcast(FP8X4), scales=w_scales[:, 0:E],
+                in_=w_grouped[:, 0].rearrange("p e c -> p (e c)"),
+            )
+            nc.vector.quantize_mx(
+                out=w_codes[:, E : 3 * E].bitcast(FP8X4), scales=w_scales[:, E : 3 * E],
+                in_=w_grouped[:, 1:3].rearrange("p w e c -> p (w e c)"),
+            )
 
         x_view = x.flatten_outer_dims().rearrange("(g p r) d -> g p r d", p=P, r=MERGE)
         q_view = out_0.flatten_outer_dims().rearrange("(g p r) e -> g p r e", p=P, r=MERGE)
         k_view = out_1.flatten_outer_dims().rearrange("(g p) e -> g p e", p=P)
         v_view = out_2.flatten_outer_dims().rearrange("(g p) e -> g p e", p=P)
-
-        x_pool = ctx.enter_context(tc.tile_pool(name="x_pool", bufs=AHEAD + 4))
-        stat_pool = ctx.enter_context(tc.tile_pool(name="stat_pool", bufs=4))
-        work = ctx.enter_context(tc.tile_pool(name="work", bufs=3))
-        t_psum = ctx.enter_context(tc.psum_pool(name="t_psum", bufs=1))
-        o_psum = ctx.enter_context(tc.psum_pool(name="o_psum", bufs=2))
 
         x_of, stats_of, moments_of, std_of, rstd_of, neg_mean_of = {}, {}, {}, {}, {}, {}
         y_of, y_t_of, planes_of, grouped_of, codes_of, scales_of, q_ps_of, kv_ps_of = {}, {}, {}, {}, {}, {}, {}, {}
@@ -133,34 +144,39 @@ def tile_siglipencoderlayer_pa_t_kernel(
                 )
             y_of[g] = y
 
-        def transpose(g):
-            y_t = [t_psum.tile([P, MERGE, P], F32, name="y_t%d" % c) for c in range(PACK)]
-            for c in range(PACK):
+        def transpose(g, half):
+            for c in (2 * half, 2 * half + 1):
+                y_t = t_psum.tile([P, MERGE, P], F32, name="y_t%d" % c)
                 for r in range(MERGE):
-                    nc.tensor.transpose(y_t[c][:, r, :], y_of[g][:, r, c * P : (c + 1) * P], ident_f32[:])
-            y_t_of[g] = y_t
+                    nc.tensor.transpose(y_t[:, r, :], y_of[g][:, r, c * P : (c + 1) * P], ident_f32[:])
+                y_t_of[(g, c)] = y_t
 
-        def scale_shift(g):
-            planes = work.tile([P, PACK, GROUP], BF16)
-            for c in range(PACK):
+        def scale_shift(g, half):
+            if half == 0:
+                planes = work.tile([P, PACK, GROUP], BF16)
+                planes_of[g] = planes
+            for c in (2 * half, 2 * half + 1):
                 nc.scalar.activation(
-                    out=planes[:, c, :], in_=y_t_of[g][c][:].rearrange("p r t -> p (r t)"), func=ACT.Identity,
+                    out=planes_of[g][:, c, :], in_=y_t_of[(g, c)][:].rearrange("p r t -> p (r t)"), func=ACT.Identity,
                     scale=gb_cols[:, c : c + 1], bias=gb_cols[:, PACK + c : PACK + c + 1],
                 )
-            planes_of[g] = planes
 
-        def regroup(g):
-            planes = planes_of[g]
+        def regrouped(g, first, count):
+            tokens = slice(first, first + count)
+            return (
+                grouped_of[g][:, tokens, :].rearrange("p (a i) c -> p a c i", i=RUN),
+                planes_of[g][:, :, tokens].rearrange("p c (a i) -> p a c i", i=RUN),
+            )
+
+        def regroup_vector(g):
             grouped = work.tile([P, GROUP, PACK], BF16, align_bytes=64)
-            nc.vector.tensor_copy(
-                out=grouped[:, 0:P, :].rearrange("p (a i) c -> p a c i", i=RUN),
-                in_=planes[:, :, 0:P].rearrange("p c (a i) -> p a c i", i=RUN),
-            )
-            nc.scalar.copy(
-                out=grouped[:, P:, :].rearrange("p (a i) c -> p a c i", i=RUN),
-                in_=planes[:, :, P:].rearrange("p c (a i) -> p a c i", i=RUN),
-            )
             grouped_of[g] = grouped
+            out, in_ = regrouped(g, 0, VECTOR_SHARE)
+            nc.vector.tensor_copy(out=out, in_=in_)
+
+        def regroup_scalar(g, half):
+            out, in_ = regrouped(g, VECTOR_SHARE + half * SCALAR_SHARE, SCALAR_SHARE)
+            nc.scalar.copy(out=out, in_=in_)
 
         def quantise(g):
             h_codes = work.tile([P, GROUP], U32, align_bytes=64)
@@ -172,25 +188,27 @@ def tile_siglipencoderlayer_pa_t_kernel(
             codes_of[g] = h_codes
             scales_of[g] = h_scales
 
-        def project(g):
-            q_ps = o_psum.tile([P, MERGE, E], F32)
-            kv_ps = o_psum.tile([P, 2, E], F32)
-            for r in range(MERGE):
+        def project(g, half):
+            if half == 0:
+                q_ps = o_psum.tile([P, MERGE, E], F32)
+                kv_ps = o_psum.tile([P, 4, E], F32)
+                q_ps_of[g] = q_ps
+                kv_ps_of[g] = kv_ps
+            kv_cols = slice(KV_FROM * E, KV_TO * E)
+            for r in (2 * half, 2 * half + 1):
                 cols = slice(r * P, (r + 1) * P)
                 nc.tensor.matmul_mx(
-                    out=q_ps[:, r, :],
+                    out=q_ps_of[g][:, r, :],
                     lhsT=codes_of[g][:, cols].bitcast(FP8X4), lhsT_scale=scales_of[g][:, cols],
                     rhs=w_codes[:, 0:E].bitcast(FP8X4), rhs_scale=w_scales[:, 0:E],
                     start=True, stop=True,
                 )
                 nc.tensor.matmul_mx(
-                    out=kv_ps[:].rearrange("p s e -> p (s e)"),
+                    out=kv_ps_of[g][:, KV_FROM:KV_TO, :].rearrange("p s e -> p (s e)"),
                     lhsT=codes_of[g][:, cols].bitcast(FP8X4), lhsT_scale=scales_of[g][:, cols],
-                    rhs=w_codes[:, E : 3 * E].bitcast(FP8X4), rhs_scale=w_scales[:, E : 3 * E],
+                    rhs=w_codes[:, kv_cols].bitcast(FP8X4), rhs_scale=w_scales[:, kv_cols],
                     start=(r == 0), stop=(r == MERGE - 1),
                 )
-            q_ps_of[g] = q_ps
-            kv_ps_of[g] = kv_ps
 
         def finish(g):
             q_sb = work.tile([P, MERGE, E], F32)
@@ -199,30 +217,38 @@ def tile_siglipencoderlayer_pa_t_kernel(
             )
             kv_sb = work.tile([P, 2, E], F32)
             nc.vector.scalar_tensor_tensor(
-                out=kv_sb[:], in0=kv_ps_of[g][:], scalar=1.0 / MERGE, in1=bias_f32[:, 1:3, :],
+                out=kv_sb[:], in0=kv_ps_of[g][:, 1:3, :], scalar=1.0 / MERGE, in1=bias_f32[:, 1:3, :],
                 op0=ALU.mult, op1=ALU.add,
             )
             nc.sync.dma_start(out=q_view[g], in_=q_sb[:])
             nc.sync.dma_start(out=k_view[g], in_=kv_sb[:, 0])
             nc.sync.dma_start(out=v_view[g], in_=kv_sb[:, 1])
 
-        def run(stage, g):
+        def run(stage, g, *half):
             if 0 <= g < GROUPS:
-                stage(g)
+                stage(g, *half)
 
         with tc.manual_schedule():
-            for g in range(AHEAD):
+            load(0)
+            load_parameters()
+            for g in range(1, AHEAD):
                 load(g)
-            for t in range(GROUPS + 7):
+            load_biases()
+            for t in range(GROUPS + LAST_LAG + 1):
                 run(load, t + AHEAD)
-                run(finish, t - 6)
-                run(regroup, t - 4)
-                run(transpose, t - 3)
+                if t == PREPARE_ROUND:
+                    prepare_parameters()
+                run(quantise, t - 6)
+                run(finish, t - LAST_LAG)
+                run(regroup_vector, t - 5)
                 run(statistics, t)
-                run(deviation, t - 1)
+                for half in range(2):
+                    run(scale_shift, t - 4, half)
+                    run(regroup_scalar, t - 5, half)
+                    run(transpose, t - 3, half)
+                    run(project, t - 7, half)
+                    if half == 0:
+                        run(deviation, t - 1)
                 run(inverse, t - 1)
                 run(aggregate, t)
                 run(normalise, t - 2)
-                run(scale_shift, t - 3)
-                run(quantise, t - 4)
-                run(project, t - 5)

@@ -24,7 +24,7 @@ GROUP = P * MERGE
 GROUPS = TOKENS // GROUP
 RUN = 4
 AHEAD = 3
-VECTOR_SHARE = P
+VECTOR_SHARE = 2 * P
 SCALAR_SHARE = (GROUP - VECTOR_SHARE) // 2
 KV_FROM, KV_TO = 0, 4
 PREPARE_ROUND = 2

@@ -24,11 +24,11 @@ GROUP = P * MERGE
 GROUPS = TOKENS // GROUP
 RUN = 4
 AHEAD = 3
-VECTOR_SHARE = 2 * P
+VECTOR_SHARE = P
 SCALAR_SHARE = (GROUP - VECTOR_SHARE) // 2
-KV_FROM, KV_TO = 0, 4
+KV_FROM, KV_TO = 1, 3
 PREPARE_ROUND = 2
-LAST_LAG = 8
+LAST_LAG = 7
 
 FLOPS = 2 * TOKENS * D * 3 * E
 
@@ -238,17 +238,16 @@ def tile_siglipencoderlayer_pa_t_kernel(
                 run(load, t + AHEAD)
                 if t == PREPARE_ROUND:
                     prepare_parameters()
-                run(quantise, t - 6)
+                run(quantise, t - 5)
+                run(regroup_vector, t - 4)
                 run(finish, t - LAST_LAG)
-                run(regroup_vector, t - 5)
-                run(statistics, t)
-                for half in range(2):
-                    run(scale_shift, t - 4, half)
-                    run(regroup_scalar, t - 5, half)
-                    run(transpose, t - 3, half)
-                    run(project, t - 7, half)
-                    if half == 0:
-                        run(deviation, t - 1)
+                run(deviation, t - 1)
                 run(inverse, t - 1)
+                run(statistics, t)
                 run(aggregate, t)
-                run(normalise, t - 2)
+                run(normalise, t - 1)
+                for half in range(2):
+                    run(scale_shift, t - 3, half)
+                    run(regroup_scalar, t - 4, half)
+                    run(transpose, t - 2, half)
+                    run(project, t - 6, half)

from contextlib import ExitStack

import concourse.mybir as mybir
from concourse.masks import make_identity

F32 = mybir.dt.float32
BF16 = mybir.dt.bfloat16
U32 = mybir.dt.uint32
U8 = mybir.dt.uint8
FP8X4 = mybir.dt.float8_e4m3fn_x4
ACT = mybir.ActivationFunctionType
ALU = mybir.AluOpType

I32 = mybir.dt.int32

P = 128
PACK = 4
TOKENS = 16 * 1024
D = P * PACK
E = 128
MERGE = 4
EPS = 1e-6
GROUP = P * MERGE
GROUPS = TOKENS // GROUP
RUN = 4
AHEAD = 3
VECTOR_SHARE = P
SCALAR_SHARE = (GROUP - VECTOR_SHARE) // 2
KV_FROM, KV_TO = 1, 3
PREPARE_ROUND = 2
LAST_LAG = 7

FLOPS = 2 * TOKENS * D * 3 * E


def tile_siglipencoderlayer_pa_t_kernel(
    tc, x, ln1_g, ln1_b, Wq, bq, Wk, bk, Wv, bv, out_0, out_1, out_2
):
    nc = tc.nc
    with ExitStack() as ctx:
        keep = ctx.enter_context(tc.tile_pool(name="keep", bufs=1))
        x_pool = ctx.enter_context(tc.tile_pool(name="x_pool", bufs=AHEAD + 4))
        stat_pool = ctx.enter_context(tc.tile_pool(name="stat_pool", bufs=4))
        work = ctx.enter_context(tc.tile_pool(name="work", bufs=3))
        t_psum = ctx.enter_context(tc.psum_pool(name="t_psum", bufs=1))
        o_psum = ctx.enter_context(tc.psum_pool(name="o_psum", bufs=2))

        ident_f32 = keep.tile([P, P], F32)
        make_identity(nc, ident_f32[:])
        ident_bf16 = keep.tile([P, P], BF16)
        make_identity(nc, ident_bf16[:])
        eps_col = keep.tile([P, 1], F32)
        nc.vector.memset(eps_col[:], EPS)

        w_rows = keep.tile([P, 3, D], BF16)
        gb_rows = keep.tile([P, P], BF16)
        nc.vector.memset(gb_rows[:], 0.0)
        bias_bf16 = keep.tile([P, 3, E], BF16)
        bias_f32 = keep.tile([P, 3, E], F32)
        w_grouped = keep.tile([P, 3, E, PACK], BF16, align_bytes=64)
        w_codes = keep.tile([P, 4 * E], U32, align_bytes=64)
        w_scales = keep.tile([P, 4 * E], U8, align_bytes=64)
        nc.vector.memset(w_codes[:, 3 * E :].bitcast(I32), 0)
        nc.vector.memset(w_scales[:, 3 * E :].bitcast(I32), 0)
        gb_cols = keep.tile([P, 2 * PACK], F32)

        def load_parameters():
            nc.sync.dma_start(out=gb_rows[0:PACK, :], in_=ln1_g.rearrange("(c p) -> c p", p=P))
            nc.sync.dma_start(out=gb_rows[PACK : 2 * PACK, :], in_=ln1_b.rearrange("(c p) -> c p", p=P))
            for w, weight in enumerate((Wq, Wk, Wv)):
                nc.sync.dma_start(out=w_rows[:, w, :], in_=weight)

        def load_biases():
            for w, bias in enumerate((bq, bk, bv)):
                nc.sync.dma_start(out=bias_bf16[:, w, :], in_=bias.partition_broadcast(P))

        def prepare_parameters():
            gb_t = o_psum.tile([P, P], BF16, tag="q_ps")
            nc.tensor.transpose(gb_t[:], gb_rows[:], ident_bf16[:])
            w_t = [o_psum.tile([P, PACK, E], BF16, name="w_t%d" % w, tag=("q_ps", "kv_ps", "kv_ps")[w]) for w in range(3)]
            for w in range(3):
                for c in range(PACK):
                    nc.tensor.transpose(w_t[w][:, c, :], w_rows[:, w, c * P : (c + 1) * P], ident_bf16[:])
            nc.vector.tensor_copy(out=gb_cols[:], in_=gb_t[:, 0 : 2 * PACK])
            for w in range(3):
                nc.vector.tensor_copy(out=w_grouped[:, w], in_=w_t[w][:].rearrange("p c e -> p e c"))
            nc.vector.tensor_copy(out=bias_f32[:], in_=bias_bf16[:])
            nc.vector.quantize_mx(
                out=w_codes[:, 0:E].bitcast(FP8X4), scales=w_scales[:, 0:E],
                in_=w_grouped[:, 0].rearrange("p e c -> p (e c)"),
            )
            nc.vector.quantize_mx(
                out=w_codes[:, E : 3 * E].bitcast(FP8X4), scales=w_scales[:, E : 3 * E],
                in_=w_grouped[:, 1:3].rearrange("p w e c -> p (w e c)"),
            )

        x_view = x.flatten_outer_dims().rearrange("(g p r) d -> g p r d", p=P, r=MERGE)
        q_view = out_0.flatten_outer_dims().rearrange("(g p r) e -> g p r e", p=P, r=MERGE)
        k_view = out_1.flatten_outer_dims().rearrange("(g p) e -> g p e", p=P)
        v_view = out_2.flatten_outer_dims().rearrange("(g p) e -> g p e", p=P)

        x_of, stats_of, moments_of, std_of, rstd_of, neg_mean_of = {}, {}, {}, {}, {}, {}
        y_of, y_t_of, planes_of, grouped_of, codes_of, scales_of, q_ps_of, kv_ps_of = {}, {}, {}, {}, {}, {}, {}, {}

        def load(g):
            x_sb = x_pool.tile([P, MERGE, D], BF16)
            nc.sync.dma_start(out=x_sb[:], in_=x_view[g])
            x_of[g] = x_sb

        def statistics(g):
            stats = stat_pool.tile([P, MERGE, 6], F32)
            for r in range(MERGE):
                nc.vector.bn_stats(out=stats[:, r, :], in_=x_of[g][:, r, :])
            stats_of[g] = stats

        def aggregate(g):
            moments = stat_pool.tile([P, MERGE, 2], F32)
            for r in range(MERGE):
                nc.vector.bn_aggr(out=moments[:, r, :], in_=stats_of[g][:, r, :])
            moments_of[g] = moments

        def deviation(g):
            std = stat_pool.tile([P, MERGE], F32)
            nc.scalar.activation(out=std[:], in_=moments_of[g][:, :, 1], func=ACT.Sqrt, bias=eps_col[:], scale=1.0)
            std_of[g] = std
            neg_mean = stat_pool.tile([P, MERGE], F32)
            nc.gpsimd.tensor_scalar(
                out=neg_mean[:], in0=moments_of[g][:, :, 0], scalar1=-1.0, scalar2=0.0, op0=ALU.mult, op1=ALU.add
            )
            neg_mean_of[g] = neg_mean

        def inverse(g):
            rstd = stat_pool.tile([P, MERGE], F32)
            nc.vector.reciprocal(out=rstd[:], in_=std_of[g][:])
            rstd_of[g] = rstd

        def normalise(g):
            y = work.tile([P, MERGE, D], F32)
            for r in range(MERGE):
                nc.gpsimd.tensor_scalar(
                    out=y[:, r, :], in0=x_of[g][:, r, :],
                    scalar1=neg_mean_of[g][:, r : r + 1], scalar2=rstd_of[g][:, r : r + 1],
                    op0=ALU.add, op1=ALU.mult,
                )
            y_of[g] = y

        def transpose(g, half):
            for c in (2 * half, 2 * half + 1):
                y_t = t_psum.tile([P, MERGE, P], F32, name="y_t%d" % c)
                for r in range(MERGE):
                    nc.tensor.transpose(y_t[:, r, :], y_of[g][:, r, c * P : (c + 1) * P], ident_f32[:])
                y_t_of[(g, c)] = y_t

        def scale_shift(g, half):
            if half == 0:
                planes = work.tile([P, PACK, GROUP], BF16)
                planes_of[g] = planes
            for c in (2 * half, 2 * half + 1):
                nc.scalar.activation(
                    out=planes_of[g][:, c, :], in_=y_t_of[(g, c)][:].rearrange("p r t -> p (r t)"), func=ACT.Identity,
                    scale=gb_cols[:, c : c + 1], bias=gb_cols[:, PACK + c : PACK + c + 1],
                )

        def regrouped(g, first, count):
            tokens = slice(first, first + count)
            return (
                grouped_of[g][:, tokens, :].rearrange("p (a i) c -> p a c i", i=RUN),
                planes_of[g][:, :, tokens].rearrange("p c (a i) -> p a c i", i=RUN),
            )

        def regroup_vector(g):
            grouped = work.tile([P, GROUP, PACK], BF16, align_bytes=64)
            grouped_of[g] = grouped
            out, in_ = regrouped(g, 0, VECTOR_SHARE)
            nc.vector.tensor_copy(out=out, in_=in_)

        def regroup_scalar(g, half):
            out, in_ = regrouped(g, VECTOR_SHARE + half * SCALAR_SHARE, SCALAR_SHARE)
            nc.scalar.copy(out=out, in_=in_)

        def quantise(g):
            h_codes = work.tile([P, GROUP], U32, align_bytes=64)
            h_scales = work.tile([P, GROUP], U8, align_bytes=64)
            nc.vector.quantize_mx(
                out=h_codes[:].bitcast(FP8X4), scales=h_scales[:],
                in_=grouped_of[g][:].rearrange("p t c -> p (t c)"),
            )
            codes_of[g] = h_codes
            scales_of[g] = h_scales

        def project(g, half):
            if half == 0:
                q_ps = o_psum.tile([P, MERGE, E], F32)
                kv_ps = o_psum.tile([P, 4, E], F32)
                q_ps_of[g] = q_ps
                kv_ps_of[g] = kv_ps
            kv_cols = slice(KV_FROM * E, KV_TO * E)
            for r in (2 * half, 2 * half + 1):
                cols = slice(r * P, (r + 1) * P)
                nc.tensor.matmul_mx(
                    out=q_ps_of[g][:, r, :],
                    lhsT=codes_of[g][:, cols].bitcast(FP8X4), lhsT_scale=scales_of[g][:, cols],
                    rhs=w_codes[:, 0:E].bitcast(FP8X4), rhs_scale=w_scales[:, 0:E],
                    start=True, stop=True,
                )
                nc.tensor.matmul_mx(
                    out=kv_ps_of[g][:, KV_FROM:KV_TO, :].rearrange("p s e -> p (s e)"),
                    lhsT=codes_of[g][:, cols].bitcast(FP8X4), lhsT_scale=scales_of[g][:, cols],
                    rhs=w_codes[:, kv_cols].bitcast(FP8X4), rhs_scale=w_scales[:, kv_cols],
                    start=(r == 0), stop=(r == MERGE - 1),
                )

        def finish(g):
            q_sb = work.tile([P, MERGE, E], F32)
            nc.vector.tensor_tensor(
                out=q_sb[:], in0=q_ps_of[g][:], in1=bias_f32[:, 0:1, :].to_broadcast([P, MERGE, E]), op=ALU.add
            )
            kv_sb = work.tile([P, 2, E], F32)
            nc.vector.scalar_tensor_tensor(
                out=kv_sb[:], in0=kv_ps_of[g][:, 1:3, :], scalar=1.0 / MERGE, in1=bias_f32[:, 1:3, :],
                op0=ALU.mult, op1=ALU.add,
            )
            nc.sync.dma_start(out=q_view[g], in_=q_sb[:])
            nc.sync.dma_start(out=k_view[g], in_=kv_sb[:, 0])
            nc.sync.dma_start(out=v_view[g], in_=kv_sb[:, 1])

        def run(stage, g, *half):
            if 0 <= g < GROUPS:
                stage(g, *half)

        with tc.manual_schedule():
            load(0)
            load_parameters()
            for g in range(1, AHEAD):
                load(g)
            load_biases()
            for t in range(GROUPS + LAST_LAG + 1):
                run(load, t + AHEAD)
                if t == PREPARE_ROUND:
                    prepare_parameters()
                run(quantise, t - 5)
                run(regroup_vector, t - 4)
                run(finish, t - LAST_LAG)
                run(deviation, t - 1)
                run(inverse, t - 1)
                run(statistics, t)
                run(aggregate, t)
                run(normalise, t - 1)
                for half in range(2):
                    run(scale_shift, t - 3, half)
                    run(regroup_scalar, t - 4, half)
                    run(transpose, t - 2, half)
                    run(project, t - 6, half)
